import numpy as np
import ml_dtypes

BF16 = ml_dtypes.bfloat16


def bf(x):
    return np.asarray(x, np.float32).astype(BF16)


def f32(x):
    return np.asarray(x, np.float32)


def f64(x):
    return np.asarray(x).astype(np.float64)


def striped(idx):
    return np.tile(idx.reshape(-1, 16).T, (8, 1))


D, M, S, N, CH = 128, 128, 2048, 1024, 32
SM_N = 1.0


def setup_inputs():
    return {"q": bf(np.random.standard_normal((D, M))), "keys": bf(np.random.standard_normal((D, S))), "offs": striped(np.random.permutation(S)[:N])}


def reference(q, keys, offs):
    idx = offs[:16].T.reshape(-1)
    s = (f64(q).T @ f64(keys)[:, idx]) * D ** -0.5
    s = s.reshape(M, N // CH, CH)
    mx = np.maximum(s.max(axis=-1, keepdims=True), 0.0)
    e = np.exp(s - mx)
    p = e / (e.sum(axis=-1, keepdims=True) + SM_N * np.exp(-mx))
    return p.reshape(M, N)

@@ -1,0 +1,74 @@
+import concourse.mybir as mybir
+
+BF16, F32, U16 = mybir.dt.bfloat16, mybir.dt.float32, mybir.dt.uint16
+ALU = mybir.AluOpType
+EXP = mybir.ActivationFunctionType.Exp
+INNERMOST = mybir.AxisListType.X
+
+D = 128
+M = 128
+S = 2048
+N = 1024
+CHUNK = 32
+PIECE = 512
+CHUNKS = PIECE // CHUNK
+SCALE = D**-0.5
+
+FLOPS = 2 * D * M * N
+
+
+def tile_hierarchicalsparseattention_kernel(tc, q, keys, offs, out):
+    nc = tc.nc
+    with (
+        tc.tile_pool(name="held", bufs=1) as held,
+        tc.tile_pool(name="work", bufs=2) as work,
+        tc.psum_pool(name="psum", bufs=2) as psum,
+    ):
+        offsets = held.tile([128, N // 16], U16, name="offsets")
+        nc.sync.dma_start(offsets[:], offs)
+        q_sb = held.tile([D, M], BF16, name="q_sb")
+        nc.scalar.dma_start(q_sb[:], q)
+        keys_sb = held.tile([D, S], BF16, name="keys_sb")
+        nc.sync.dma_start(keys_sb[:], keys)
+
+        for piece in range(N // PIECE):
+            piece_offsets = offsets[:, piece * (PIECE // 16) : (piece + 1) * (PIECE // 16)]
+            scores = psum.tile([M, PIECE], F32, name="scores")
+            nc.tensor.matmul(scores[:], q_sb[:], keys_sb[:].indirect(piece_offsets), start=True, stop=True)
+            scores_by_chunk = scores[:].rearrange("m (t c) -> m t c", c=CHUNK)
+
+            chunk_max = work.tile([M, CHUNKS], F32, name="chunk_max")
+            nc.vector.tensor_reduce(out=chunk_max[:], in_=scores_by_chunk, axis=INNERMOST, op=ALU.max)
+            neg_max = work.tile([M, CHUNKS], F32, name="neg_max")
+            nc.vector.tensor_scalar(
+                out=neg_max[:], in0=chunk_max[:], scalar1=0.0, scalar2=-1.0, op0=ALU.max, op1=ALU.mult
+            )
+            neg_max_column = neg_max[:].unsqueeze(2)
+
+            shifted = work.tile([M, PIECE], F32, name="shifted")
+            shifted_by_chunk = shifted[:].rearrange("m (t c) -> m t c", c=CHUNK)
+            nc.vector.tensor_tensor(
+                out=shifted_by_chunk,
+                in0=scores_by_chunk,
+                in1=neg_max_column.to_broadcast([M, CHUNKS, CHUNK]),
+                op=ALU.add,
+            )
+
+            exps = work.tile([M, CHUNKS * (CHUNK + 1)], F32, name="exps")
+            exps_by_chunk = exps[:].rearrange("m (t c) -> m t c", c=CHUNK + 1)
+            nc.scalar.activation(out=exps_by_chunk[:, :, CHUNK : CHUNK + 1], in_=neg_max_column, func=EXP, scale=SCALE)
+            nc.scalar.activation(out=exps_by_chunk[:, :, 0:CHUNK], in_=shifted_by_chunk, func=EXP, scale=SCALE)
+
+            denominator = work.tile([M, CHUNKS], F32, name="denominator")
+            nc.vector.tensor_reduce(out=denominator[:], in_=exps_by_chunk, axis=INNERMOST, op=ALU.add)
+            inverse = work.tile([M, CHUNKS], F32, name="inverse")
+            nc.vector.reciprocal(inverse[:], denominator[:])
+
+            probs = work.tile([M, PIECE], F32, name="probs")
+            nc.vector.tensor_tensor(
+                out=probs[:].rearrange("m (t c) -> m t c", c=CHUNK),
+                in0=exps_by_chunk[:, :, 0:CHUNK],
+                in1=inverse[:].unsqueeze(2).to_broadcast([M, CHUNKS, CHUNK]),
+                op=ALU.mult,
+            )
+            nc.sync.dma_start(out[:, piece * PIECE : (piece + 1) * PIECE], probs[:])

@@ -10,7 +10,8 @@ M = 128
 S = 2048
 N = 1024
 CHUNK = 32
-PIECE = 512
+PIECE = 256
+PIECES = N // PIECE
 CHUNKS = PIECE // CHUNK
 SCALE = D**-0.5
 
@@ -21,8 +22,8 @@ def tile_hierarchicalsparseattention_kernel(tc, q, keys, offs, out):
     nc = tc.nc
     with (
         tc.tile_pool(name="held", bufs=1) as held,
-        tc.tile_pool(name="work", bufs=2) as work,
-        tc.psum_pool(name="psum", bufs=2) as psum,
+        tc.tile_pool(name="work", bufs=PIECES) as work,
+        tc.psum_pool(name="psum", bufs=PIECES) as psum,
     ):
         offsets = held.tile([128, N // 16], U16, name="offsets")
         nc.sync.dma_start(offsets[:], offs)
@@ -31,7 +32,7 @@ def tile_hierarchicalsparseattention_kernel(tc, q, keys, offs, out):
         keys_sb = held.tile([D, S], BF16, name="keys_sb")
         nc.sync.dma_start(keys_sb[:], keys)
 
-        for piece in range(N // PIECE):
+        for piece in range(PIECES):
             piece_offsets = offsets[:, piece * (PIECE // 16) : (piece + 1) * (PIECE // 16)]
             scores = psum.tile([M, PIECE], F32, name="scores")
             nc.tensor.matmul(scores[:], q_sb[:], keys_sb[:].indirect(piece_offsets), start=True, stop=True)
@@ -39,25 +40,22 @@ def tile_hierarchicalsparseattention_kernel(tc, q, keys, offs, out):
 
             chunk_max = work.tile([M, CHUNKS], F32, name="chunk_max")
             nc.vector.tensor_reduce(out=chunk_max[:], in_=scores_by_chunk, axis=INNERMOST, op=ALU.max)
-            neg_max = work.tile([M, CHUNKS], F32, name="neg_max")
+            shift = work.tile([M, CHUNKS], F32, name="shift")
             nc.vector.tensor_scalar(
-                out=neg_max[:], in0=chunk_max[:], scalar1=0.0, scalar2=-1.0, op0=ALU.max, op1=ALU.mult
-            )
-            neg_max_column = neg_max[:].unsqueeze(2)
-
-            shifted = work.tile([M, PIECE], F32, name="shifted")
-            shifted_by_chunk = shifted[:].rearrange("m (t c) -> m t c", c=CHUNK)
-            nc.vector.tensor_tensor(
-                out=shifted_by_chunk,
-                in0=scores_by_chunk,
-                in1=neg_max_column.to_broadcast([M, CHUNKS, CHUNK]),
-                op=ALU.add,
+                out=shift[:], in0=chunk_max[:], scalar1=0.0, scalar2=-SCALE, op0=ALU.max, op1=ALU.mult
             )
 
             exps = work.tile([M, CHUNKS * (CHUNK + 1)], F32, name="exps")
             exps_by_chunk = exps[:].rearrange("m (t c) -> m t c", c=CHUNK + 1)
-            nc.scalar.activation(out=exps_by_chunk[:, :, CHUNK : CHUNK + 1], in_=neg_max_column, func=EXP, scale=SCALE)
-            nc.scalar.activation(out=exps_by_chunk[:, :, 0:CHUNK], in_=shifted_by_chunk, func=EXP, scale=SCALE)
+            nc.scalar.activation(out=exps_by_chunk[:, :, CHUNK : CHUNK + 1], in_=shift[:].unsqueeze(2), func=EXP)
+            for t in range(CHUNKS):
+                nc.scalar.activation(
+                    out=exps_by_chunk[:, t, 0:CHUNK],
+                    in_=scores_by_chunk[:, t, :],
+                    func=EXP,
+                    bias=shift[:, t : t + 1],
+                    scale=SCALE,
+                )
 
             denominator = work.tile([M, CHUNKS], F32, name="denominator")
             nc.vector.tensor_reduce(out=denominator[:], in_=exps_by_chunk, axis=INNERMOST, op=ALU.add)

@@ -45,27 +45,30 @@ def tile_hierarchicalsparseattention_kernel(tc, q, keys, offs, out):
                 out=shift[:], in0=chunk_max[:], scalar1=0.0, scalar2=-SCALE, op0=ALU.max, op1=ALU.mult
             )
 
-            exps = work.tile([M, CHUNKS * (CHUNK + 1)], F32, name="exps")
-            exps_by_chunk = exps[:].rearrange("m (t c) -> m t c", c=CHUNK + 1)
-            nc.scalar.activation(out=exps_by_chunk[:, :, CHUNK : CHUNK + 1], in_=shift[:].unsqueeze(2), func=EXP)
+            exps = work.tile([M, PIECE], F32, name="exps")
+            exps_by_chunk = exps[:].rearrange("m (t c) -> m t c", c=CHUNK)
+            chunk_sum = work.tile([M, CHUNKS], F32, name="chunk_sum")
             for t in range(CHUNKS):
                 nc.scalar.activation(
-                    out=exps_by_chunk[:, t, 0:CHUNK],
+                    out=exps_by_chunk[:, t, :],
                     in_=scores_by_chunk[:, t, :],
                     func=EXP,
                     bias=shift[:, t : t + 1],
                     scale=SCALE,
+                    accum_out=chunk_sum[:, t : t + 1],
                 )
+            extra_term = work.tile([M, CHUNKS], F32, name="extra_term")
+            nc.scalar.activation(out=extra_term[:], in_=shift[:], func=EXP)
 
             denominator = work.tile([M, CHUNKS], F32, name="denominator")
-            nc.vector.tensor_reduce(out=denominator[:], in_=exps_by_chunk, axis=INNERMOST, op=ALU.add)
+            nc.vector.tensor_tensor(out=denominator[:], in0=chunk_sum[:], in1=extra_term[:], op=ALU.add)
             inverse = work.tile([M, CHUNKS], F32, name="inverse")
             nc.vector.reciprocal(inverse[:], denominator[:])
 
             probs = work.tile([M, PIECE], F32, name="probs")
             nc.vector.tensor_tensor(
                 out=probs[:].rearrange("m (t c) -> m t c", c=CHUNK),
-                in0=exps_by_chunk[:, :, 0:CHUNK],
+                in0=exps_by_chunk,
                 in1=inverse[:].unsqueeze(2).to_broadcast([M, CHUNKS, CHUNK]),
                 op=ALU.mult,
             )

@@ -15,6 +15,9 @@ PIECES = N // PIECE
 CHUNKS = PIECE // CHUNK
 SCALE = D**-0.5
 
+WARM_COLUMNS = 512
+WARM_MATMULS = 8
+
 FLOPS = 2 * D * M * N
 
 
@@ -24,6 +27,7 @@ def tile_hierarchicalsparseattention_kernel(tc, q, keys, offs, out):
         tc.tile_pool(name="held", bufs=1) as held,
         tc.tile_pool(name="work", bufs=PIECES) as work,
         tc.psum_pool(name="psum", bufs=PIECES) as psum,
+        tc.psum_pool(name="warm_psum", bufs=1) as warm_psum,
     ):
         offsets = held.tile([128, N // 16], U16, name="offsets")
         nc.sync.dma_start(offsets[:], offs)
@@ -31,6 +35,12 @@ def tile_hierarchicalsparseattention_kernel(tc, q, keys, offs, out):
         nc.scalar.dma_start(q_sb[:], q)
         keys_sb = held.tile([D, S], BF16, name="keys_sb")
         nc.sync.dma_start(keys_sb[:], keys)
+
+        zeros = held.tile([D, WARM_COLUMNS], BF16, name="zeros")
+        nc.vector.memset(zeros[:], 0.0)
+        unread = warm_psum.tile([M, WARM_COLUMNS], F32, name="unread")
+        for repeat in range(WARM_MATMULS):
+            nc.tensor.matmul(unread[:], zeros[:, 0:M], zeros[:], start=True, stop=True)
 
         for piece in range(PIECES):
             piece_offsets = offsets[:, piece * (PIECE // 16) : (piece + 1) * (PIECE // 16)]
@@ -45,30 +55,27 @@ def tile_hierarchicalsparseattention_kernel(tc, q, keys, offs, out):
                 out=shift[:], in0=chunk_max[:], scalar1=0.0, scalar2=-SCALE, op0=ALU.max, op1=ALU.mult
             )
 
-            exps = work.tile([M, PIECE], F32, name="exps")
-            exps_by_chunk = exps[:].rearrange("m (t c) -> m t c", c=CHUNK)
-            chunk_sum = work.tile([M, CHUNKS], F32, name="chunk_sum")
+            exps = work.tile([M, CHUNKS * (CHUNK + 1)], F32, name="exps")
+            exps_by_chunk = exps[:].rearrange("m (t c) -> m t c", c=CHUNK + 1)
+            nc.scalar.activation(out=exps_by_chunk[:, :, CHUNK : CHUNK + 1], in_=shift[:].unsqueeze(2), func=EXP)
             for t in range(CHUNKS):
                 nc.scalar.activation(
-                    out=exps_by_chunk[:, t, :],
+                    out=exps_by_chunk[:, t, 0:CHUNK],
                     in_=scores_by_chunk[:, t, :],
                     func=EXP,
                     bias=shift[:, t : t + 1],
                     scale=SCALE,
-                    accum_out=chunk_sum[:, t : t + 1],
                 )
-            extra_term = work.tile([M, CHUNKS], F32, name="extra_term")
-            nc.scalar.activation(out=extra_term[:], in_=shift[:], func=EXP)
 
             denominator = work.tile([M, CHUNKS], F32, name="denominator")
-            nc.vector.tensor_tensor(out=denominator[:], in0=chunk_sum[:], in1=extra_term[:], op=ALU.add)
+            nc.vector.tensor_reduce(out=denominator[:], in_=exps_by_chunk, axis=INNERMOST, op=ALU.add)
             inverse = work.tile([M, CHUNKS], F32, name="inverse")
             nc.vector.reciprocal(inverse[:], denominator[:])
 
             probs = work.tile([M, PIECE], F32, name="probs")
             nc.vector.tensor_tensor(
                 out=probs[:].rearrange("m (t c) -> m t c", c=CHUNK),
-                in0=exps_by_chunk,
+                in0=exps_by_chunk[:, :, 0:CHUNK],
                 in1=inverse[:].unsqueeze(2).to_broadcast([M, CHUNKS, CHUNK]),
                 op=ALU.mult,
             )

@@ -10,13 +10,9 @@ M = 128
 S = 2048
 N = 1024
 CHUNK = 32
-PIECE = 256
-PIECES = N // PIECE
-CHUNKS = PIECE // CHUNK
 SCALE = D**-0.5
-
-WARM_COLUMNS = 512
-WARM_MATMULS = 8
+PIECE_WIDTHS = (128, 256, 256, 256, 128)
+assert sum(PIECE_WIDTHS) == N and all(width % CHUNK == 0 for width in PIECE_WIDTHS)
 
 FLOPS = 2 * D * M * N
 
@@ -25,40 +21,37 @@ def tile_hierarchicalsparseattention_kernel(tc, q, keys, offs, out):
     nc = tc.nc
     with (
         tc.tile_pool(name="held", bufs=1) as held,
-        tc.tile_pool(name="work", bufs=PIECES) as work,
-        tc.psum_pool(name="psum", bufs=PIECES) as psum,
-        tc.psum_pool(name="warm_psum", bufs=1) as warm_psum,
+        tc.tile_pool(name="work", bufs=len(PIECE_WIDTHS)) as work,
+        tc.psum_pool(name="psum", bufs=len(PIECE_WIDTHS)) as psum,
     ):
         offsets = held.tile([128, N // 16], U16, name="offsets")
-        nc.sync.dma_start(offsets[:], offs)
-        q_sb = held.tile([D, M], BF16, name="q_sb")
-        nc.scalar.dma_start(q_sb[:], q)
         keys_sb = held.tile([D, S], BF16, name="keys_sb")
+        q_sb = held.tile([D, M], BF16, name="q_sb")
         nc.sync.dma_start(keys_sb[:], keys)
+        nc.sync.dma_start(offsets[:], offs)
+        nc.scalar.dma_start(q_sb[:], q)
 
-        zeros = held.tile([D, WARM_COLUMNS], BF16, name="zeros")
-        nc.vector.memset(zeros[:], 0.0)
-        unread = warm_psum.tile([M, WARM_COLUMNS], F32, name="unread")
-        for repeat in range(WARM_MATMULS):
-            nc.tensor.matmul(unread[:], zeros[:, 0:M], zeros[:], start=True, stop=True)
+        exps_of_piece = []
+        first = 0
+        for width in PIECE_WIDTHS:
+            chunks = width // CHUNK
 
-        for piece in range(PIECES):
-            piece_offsets = offsets[:, piece * (PIECE // 16) : (piece + 1) * (PIECE // 16)]
-            scores = psum.tile([M, PIECE], F32, name="scores")
+            piece_offsets = offsets[:, first // 16 : (first + width) // 16]
+            scores = psum.tile([M, width], F32, name="scores")
             nc.tensor.matmul(scores[:], q_sb[:], keys_sb[:].indirect(piece_offsets), start=True, stop=True)
             scores_by_chunk = scores[:].rearrange("m (t c) -> m t c", c=CHUNK)
 
-            chunk_max = work.tile([M, CHUNKS], F32, name="chunk_max")
+            chunk_max = work.tile([M, chunks], F32, name="chunk_max")
             nc.vector.tensor_reduce(out=chunk_max[:], in_=scores_by_chunk, axis=INNERMOST, op=ALU.max)
-            shift = work.tile([M, CHUNKS], F32, name="shift")
+            shift = work.tile([M, chunks], F32, name="shift")
             nc.vector.tensor_scalar(
                 out=shift[:], in0=chunk_max[:], scalar1=0.0, scalar2=-SCALE, op0=ALU.max, op1=ALU.mult
             )
 
-            exps = work.tile([M, CHUNKS * (CHUNK + 1)], F32, name="exps")
+            exps = work.tile([M, chunks * (CHUNK + 1)], F32, name="exps")
             exps_by_chunk = exps[:].rearrange("m (t c) -> m t c", c=CHUNK + 1)
             nc.scalar.activation(out=exps_by_chunk[:, :, CHUNK : CHUNK + 1], in_=shift[:].unsqueeze(2), func=EXP)
-            for t in range(CHUNKS):
+            for t in range(chunks):
                 nc.scalar.activation(
                     out=exps_by_chunk[:, t, 0:CHUNK],
                     in_=scores_by_chunk[:, t, :],
@@ -67,16 +60,23 @@ def tile_hierarchicalsparseattention_kernel(tc, q, keys, offs, out):
                     scale=SCALE,
                 )
 
-            denominator = work.tile([M, CHUNKS], F32, name="denominator")
+            exps_of_piece.append(exps_by_chunk)
+            first += width
+
+        first = 0
+        for width, exps_by_chunk in zip(PIECE_WIDTHS, exps_of_piece):
+            chunks = width // CHUNK
+            denominator = work.tile([M, chunks], F32, name="denominator")
             nc.vector.tensor_reduce(out=denominator[:], in_=exps_by_chunk, axis=INNERMOST, op=ALU.add)
-            inverse = work.tile([M, CHUNKS], F32, name="inverse")
+            inverse = work.tile([M, chunks], F32, name="inverse")
             nc.vector.reciprocal(inverse[:], denominator[:])
 
-            probs = work.tile([M, PIECE], F32, name="probs")
+            probs = work.tile([M, width], F32, name="probs")
             nc.vector.tensor_tensor(
                 out=probs[:].rearrange("m (t c) -> m t c", c=CHUNK),
                 in0=exps_by_chunk[:, :, 0:CHUNK],
-                in1=inverse[:].unsqueeze(2).to_broadcast([M, CHUNKS, CHUNK]),
+                in1=inverse[:].unsqueeze(2).to_broadcast([M, chunks, CHUNK]),
                 op=ALU.mult,
             )
-            nc.sync.dma_start(out[:, piece * PIECE : (piece + 1) * PIECE], probs[:])
+            nc.sync.dma_start(out[:, first : first + width], probs[:])
+            first += width

@@ -11,7 +11,7 @@ S = 2048
 N = 1024
 CHUNK = 32
 SCALE = D**-0.5
-PIECE_WIDTHS = (128, 256, 256, 256, 128)
+PIECE_WIDTHS = (64, 192, 256, 256, 192, 64)
 assert sum(PIECE_WIDTHS) == N and all(width % CHUNK == 0 for width in PIECE_WIDTHS)
 
 FLOPS = 2 * D * M * N

@@ -11,7 +11,8 @@ S = 2048
 N = 1024
 CHUNK = 32
 SCALE = D**-0.5
-PIECE_WIDTHS = (64, 192, 256, 256, 192, 64)
+PIECE_WIDTHS = (128, 256, 256, 256, 128)
+PIECES_FINISHED_ON_GPSIMD = 2
 assert sum(PIECE_WIDTHS) == N and all(width % CHUNK == 0 for width in PIECE_WIDTHS)
 
 FLOPS = 2 * D * M * N
@@ -64,15 +65,17 @@ def tile_hierarchicalsparseattention_kernel(tc, q, keys, offs, out):
             first += width
 
         first = 0
-        for width, exps_by_chunk in zip(PIECE_WIDTHS, exps_of_piece):
+        for piece, (width, exps_by_chunk) in enumerate(zip(PIECE_WIDTHS, exps_of_piece)):
             chunks = width // CHUNK
             denominator = work.tile([M, chunks], F32, name="denominator")
             nc.vector.tensor_reduce(out=denominator[:], in_=exps_by_chunk, axis=INNERMOST, op=ALU.add)
             inverse = work.tile([M, chunks], F32, name="inverse")
             nc.vector.reciprocal(inverse[:], denominator[:])
 
+            on_gpsimd = piece < PIECES_FINISHED_ON_GPSIMD
+            multiplier = nc.gpsimd if on_gpsimd else nc.vector
             probs = work.tile([M, width], F32, name="probs")
-            nc.vector.tensor_tensor(
+            multiplier.tensor_tensor(
                 out=probs[:].rearrange("m (t c) -> m t c", c=CHUNK),
                 in0=exps_by_chunk[:, :, 0:CHUNK],
                 in1=inverse[:].unsqueeze(2).to_broadcast([M, chunks, CHUNK]),

@@ -11,6 +11,7 @@ S = 2048
 N = 1024
 CHUNK = 32
 SCALE = D**-0.5
+PITCH = CHUNK + 4
 PIECE_WIDTHS = (128, 256, 256, 256, 128)
 PIECES_FINISHED_ON_GPSIMD = 2
 assert sum(PIECE_WIDTHS) == N and all(width % CHUNK == 0 for width in PIECE_WIDTHS)
@@ -49,8 +50,8 @@ def tile_hierarchicalsparseattention_kernel(tc, q, keys, offs, out):
                 out=shift[:], in0=chunk_max[:], scalar1=0.0, scalar2=-SCALE, op0=ALU.max, op1=ALU.mult
             )
 
-            exps = work.tile([M, chunks * (CHUNK + 1)], F32, name="exps")
-            exps_by_chunk = exps[:].rearrange("m (t c) -> m t c", c=CHUNK + 1)
+            exps = work.tile([M, chunks * PITCH], F32, name="exps")
+            exps_by_chunk = exps[:].rearrange("m (t c) -> m t c", c=PITCH)
             nc.scalar.activation(out=exps_by_chunk[:, :, CHUNK : CHUNK + 1], in_=shift[:].unsqueeze(2), func=EXP)
             for t in range(chunks):
                 nc.scalar.activation(
@@ -68,7 +69,7 @@ def tile_hierarchicalsparseattention_kernel(tc, q, keys, offs, out):
         for piece, (width, exps_by_chunk) in enumerate(zip(PIECE_WIDTHS, exps_of_piece)):
             chunks = width // CHUNK
             denominator = work.tile([M, chunks], F32, name="denominator")
-            nc.vector.tensor_reduce(out=denominator[:], in_=exps_by_chunk, axis=INNERMOST, op=ALU.add)
+            nc.vector.tensor_reduce(out=denominator[:], in_=exps_by_chunk[:, :, 0 : CHUNK + 1], axis=INNERMOST, op=ALU.add)
             inverse = work.tile([M, chunks], F32, name="inverse")
             nc.vector.reciprocal(inverse[:], denominator[:])
 

import concourse.mybir as mybir

BF16, F32, U16 = mybir.dt.bfloat16, mybir.dt.float32, mybir.dt.uint16
ALU = mybir.AluOpType
EXP = mybir.ActivationFunctionType.Exp
INNERMOST = mybir.AxisListType.X

D = 128
M = 128
S = 2048
N = 1024
CHUNK = 32
SCALE = D**-0.5
PITCH = CHUNK + 4
PIECE_WIDTHS = (128, 256, 256, 256, 128)
PIECES_FINISHED_ON_GPSIMD = 2
assert sum(PIECE_WIDTHS) == N and all(width % CHUNK == 0 for width in PIECE_WIDTHS)

FLOPS = 2 * D * M * N


def tile_hierarchicalsparseattention_kernel(tc, q, keys, offs, out):
    nc = tc.nc
    with (
        tc.tile_pool(name="held", bufs=1) as held,
        tc.tile_pool(name="work", bufs=len(PIECE_WIDTHS)) as work,
        tc.psum_pool(name="psum", bufs=len(PIECE_WIDTHS)) as psum,
    ):
        offsets = held.tile([128, N // 16], U16, name="offsets")
        keys_sb = held.tile([D, S], BF16, name="keys_sb")
        q_sb = held.tile([D, M], BF16, name="q_sb")
        nc.sync.dma_start(keys_sb[:], keys)
        nc.sync.dma_start(offsets[:], offs)
        nc.scalar.dma_start(q_sb[:], q)

        exps_of_piece = []
        first = 0
        for width in PIECE_WIDTHS:
            chunks = width // CHUNK

            piece_offsets = offsets[:, first // 16 : (first + width) // 16]
            scores = psum.tile([M, width], F32, name="scores")
            nc.tensor.matmul(scores[:], q_sb[:], keys_sb[:].indirect(piece_offsets), start=True, stop=True)
            scores_by_chunk = scores[:].rearrange("m (t c) -> m t c", c=CHUNK)

            chunk_max = work.tile([M, chunks], F32, name="chunk_max")
            nc.vector.tensor_reduce(out=chunk_max[:], in_=scores_by_chunk, axis=INNERMOST, op=ALU.max)
            shift = work.tile([M, chunks], F32, name="shift")
            nc.vector.tensor_scalar(
                out=shift[:], in0=chunk_max[:], scalar1=0.0, scalar2=-SCALE, op0=ALU.max, op1=ALU.mult
            )

            exps = work.tile([M, chunks * PITCH], F32, name="exps")
            exps_by_chunk = exps[:].rearrange("m (t c) -> m t c", c=PITCH)
            nc.scalar.activation(out=exps_by_chunk[:, :, CHUNK : CHUNK + 1], in_=shift[:].unsqueeze(2), func=EXP)
            for t in range(chunks):
                nc.scalar.activation(
                    out=exps_by_chunk[:, t, 0:CHUNK],
                    in_=scores_by_chunk[:, t, :],
                    func=EXP,
                    bias=shift[:, t : t + 1],
                    scale=SCALE,
                )

            exps_of_piece.append(exps_by_chunk)
            first += width

        first = 0
        for piece, (width, exps_by_chunk) in enumerate(zip(PIECE_WIDTHS, exps_of_piece)):
            chunks = width // CHUNK
            denominator = work.tile([M, chunks], F32, name="denominator")
            nc.vector.tensor_reduce(out=denominator[:], in_=exps_by_chunk[:, :, 0 : CHUNK + 1], axis=INNERMOST, op=ALU.add)
            inverse = work.tile([M, chunks], F32, name="inverse")
            nc.vector.reciprocal(inverse[:], denominator[:])

            on_gpsimd = piece < PIECES_FINISHED_ON_GPSIMD
            multiplier = nc.gpsimd if on_gpsimd else nc.vector
            probs = work.tile([M, width], F32, name="probs")
            multiplier.tensor_tensor(
                out=probs[:].rearrange("m (t c) -> m t c", c=CHUNK),
                in0=exps_by_chunk[:, :, 0:CHUNK],
                in1=inverse[:].unsqueeze(2).to_broadcast([M, chunks, CHUNK]),
                op=ALU.mult,
            )
            nc.sync.dma_start(out[:, first : first + width], probs[:])
            first += width
